import numpy as np
import ml_dtypes


def mxq(x, axis, fmt="e4m3"):
    dtype, down = {"e4m3": (ml_dtypes.float8_e4m3fn, 7), "e5m2": (ml_dtypes.float8_e5m2, 14)}[fmt]
    v = np.moveaxis(np.asarray(x, np.float32).astype(ml_dtypes.bfloat16).astype(np.float64), axis, -1)
    blocks = v.reshape(v.shape[:-1] + (-1, 32))
    amax = np.abs(blocks).max(-1, keepdims=True)
    byte = np.maximum(np.where(amax > 0, np.frexp(amax)[1] - 1 + 127, 0) - down, 1)
    scale = np.exp2(byte - 127.0)
    codes = (blocks / scale).astype(np.float32).astype(dtype).astype(np.float64)
    return np.moveaxis((codes * scale).reshape(v.shape), -1, axis)


WIDE = False


def mx_kscale(k):
    if not WIDE:
        return np.ones(k)
    levels = np.array([10, -10, 5, -5, 0])
    if k % 512:
        return np.exp2(np.random.permutation(np.resize(levels, k // 32))).repeat(32)
    a = np.empty((k // 512, 16))
    for p in range(k // 512):
        a[p, :8] = np.random.permutation(np.resize(levels, 8))
        for g in range(8):
            far = levels[np.abs(levels - a[p, g]) >= 10]
            a[p, g + 8] = far[np.random.randint(len(far))]
    return np.exp2(a.ravel()).repeat(32)


BF16 = ml_dtypes.bfloat16


def bf(x):
    return np.asarray(x, np.float32).astype(BF16)


def f64(x):
    return np.asarray(x).astype(np.float64)


T, D, F1, F2 = 512, 1024, 4096, 1024
EPS = 1e-3


def _layernorm(x, gamma, beta):
    mu = np.mean(x, axis=-1, keepdims=True)
    var = np.mean(np.square(x - mu), axis=-1, keepdims=True)
    rsigma = 1.0 / np.sqrt(var + EPS)
    return (x - mu) * rsigma * gamma + beta


def _gelu_tanh(x):
    c = 0.7978845608028654
    return 0.5 * x * (1.0 + np.tanh(c * (x + 0.044715 * x * x * x)))


def setup_inputs():
    s = mx_kscale(D)
    t = mx_kscale(F1)
    u = np.minimum(t, 1.0 / t) ** 2
    return {"inputs": bf(np.random.standard_normal((T, D)) + 0.5),
            "gamma": bf((1.0 + 0.1 * np.random.standard_normal(D)) * s),
            "beta": bf(0.1 * np.random.standard_normal(D) * s),
            "fc1_kernel": bf(np.random.standard_normal((D, F1)) / np.sqrt(D) / s[:, None] * u[None, :]),
            "fc1_bias": bf(0.1 * np.random.standard_normal(F1) * u),
            "fc2_kernel": bf(np.random.standard_normal((F1, F2)) * 1.5 / np.sqrt(F1) / u[:, None]),
            "fc2_bias": bf(0.1 * np.random.standard_normal(F2))}


def reference(inputs, gamma, beta, fc1_kernel, fc1_bias, fc2_kernel, fc2_bias):
    ln_out = _layernorm(f64(inputs), f64(gamma), f64(beta))
    fc1_out = (mxq(ln_out, 1, "e4m3") @ mxq(f64(fc1_kernel), 0, "e4m3")) + f64(fc1_bias)
    gelu_out = _gelu_tanh(fc1_out)
    fc2_out = (mxq(gelu_out, 1, "e4m3") @ mxq(f64(fc2_kernel), 0, "e4m3")) + f64(fc2_bias)
    return fc2_out

@@ -1,0 +1,437 @@
+from contextlib import ExitStack
+
+import concourse.mybir as mybir
+from concourse.masks import make_identity
+
+F32 = mybir.dt.float32
+BF16 = mybir.dt.bfloat16
+U32 = mybir.dt.uint32
+U8 = mybir.dt.uint8
+FP8X4 = mybir.dt.float8_e4m3fn_x4
+ACT = mybir.ActivationFunctionType
+ALU = mybir.AluOpType
+
+P = 128
+T = 512
+D = 1024
+F1 = 4096
+F2 = 1024
+EPS = 1e-3
+FLOPS = 2 * T * D * F1 + 2 * T * F1 * F2
+
+JW = 1024
+RING = 12
+BLOCKS = [[0,512],[512,256],[768,256]]
+XS = [1008,912,384,560,1024,1024,752,544,368,400,400,112,384,272,304,0]
+QSPLIT = {15: [[0,2],[2,3],[3,4]]}
+LOOK_S = 1
+LOOK_V = 1
+DG = 2
+DH = 3
+XH_ON = "SSSS"
+EV_ON = "SSVVSSVV"
+EV_ORDER = [0,2,1,3,4,6,5,7]
+V_SEQ = ["p","ppppqpp","q"]
+S_SEQ = ["p","","p"]
+CUTS = {"V": {0: 256}, "S": {0: 256}}
+COD_BUFS = 4
+Q_COLS = 512
+GRP_BUFS = 5
+FIN_DELAY = 1
+PINNED = True
+
+
+def make_jobs():
+    jobs = []
+    for q in range(8):
+        jobs.append({"kind": 1, "width": 512, "segs": [(q, 0), (q, 1)]})
+    for bi, (c0, width) in enumerate(BLOCKS):
+        per = JW // width
+        for g0 in range(0, 8, per):
+            jobs.append(
+                {"kind": 2, "block": bi, "c0": c0, "width": width,
+                 "segs": [(8 + g, g) for g in range(g0, g0 + per)]}
+            )
+    return jobs
+
+
+def tile_layernormmlp_kernel(
+    tc, inputs, gamma, beta, fc1_kernel, fc1_bias, fc2_kernel, fc2_bias, out
+):
+    nc = tc.nc
+    jobs = make_jobs()
+    n_jobs = len(jobs)
+    last_use = {}
+    for ji, job in enumerate(jobs):
+        for k, sub in job["segs"]:
+            last_use[k] = ji
+    with ExitStack() as ctx:
+        const = ctx.enter_context(tc.tile_pool(name="const", bufs=1))
+        ring = ctx.enter_context(tc.tile_pool(name="ring", bufs=RING))
+        grpp = ctx.enter_context(tc.tile_pool(name="grpp", bufs=GRP_BUFS))
+        codp = ctx.enter_context(tc.tile_pool(name="codp", bufs=COD_BUFS))
+        hpp = ctx.enter_context(tc.tile_pool(name="hpp", bufs=3))
+        hgp = ctx.enter_context(tc.tile_pool(name="hgp", bufs=2))
+        outp = ctx.enter_context(tc.tile_pool(name="outp", bufs=4))
+        psum = ctx.enter_context(tc.psum_pool(name="psum", bufs=1))
+        if PINNED:
+            ctx.enter_context(tc.manual_schedule())
+
+        def regroup_part(copy_fn, dst, src):
+            copy_fn(
+                out=dst.rearrange("p (c i) t -> p c t i", i=4),
+                in_=src.rearrange("p t (c i) -> p c t i", i=4),
+            )
+
+        def quantise(codes, scales, grouped, cols):
+            for a in range(0, cols, min(cols, Q_COLS)):
+                b = a + min(cols, Q_COLS)
+                nc.vector.quantize_mx(
+                    out=codes[:, a:b].bitcast(FP8X4), scales=scales[:, a:b],
+                    in_=grouped[:, a:b, :].rearrange("p w t -> p (w t)"),
+                )
+
+        ident_b = const.tile([P, P], BF16, name="ident_b")
+        make_identity(nc, ident_b[:])
+        ident_f = const.tile([P, P], F32, name="ident_f")
+        make_identity(nc, ident_f[:])
+        eps_t = const.tile([P, 1], F32, name="eps_t")
+        nc.vector.memset(eps_t[:], EPS)
+        vec = const.tile([P, 512], BF16, name="vec")
+        nc.vector.memset(vec[:], 0.0)
+
+        x_all = ring.tile([P, 4, D], BF16, name="x_all", tag="ring")
+        for i in range(4):
+            nc.sync.dma_start(out=x_all[:, i, :], in_=inputs[i * P : (i + 1) * P, :])
+        nc.scalar.dma_start(out=vec[0:2, :], in_=gamma.rearrange("(r c) -> r c", c=512))
+        nc.scalar.dma_start(out=vec[2:4, :], in_=beta.rearrange("(r c) -> r c", c=512))
+        nc.scalar.dma_start(out=vec[4:12, :], in_=fc1_bias.rearrange("(r c) -> r c", c=512))
+        warm = const.tile([P, 2], F32, name="warm")
+        nc.scalar.activation(out=warm[:, 0:1], in_=eps_t[:], func=ACT.Sqrt)
+
+        raw = {}
+        done = {"S": 0, "V": 0, "load": 0, "free": 0, "quant": 0}
+
+        def load(k):
+            if k < 8:
+                t = ring.tile([P, 8, 512], BF16, name="raw", tag="ring")
+                for c in range(2):
+                    nc.sync.dma_start(
+                        out=t[:, 4 * c : 4 * c + 4, :],
+                        in_=fc1_kernel[c * 512 : (c + 1) * 512, k * 512 : (k + 1) * 512].rearrange(
+                            "(p j) f -> p j f", j=4
+                        ),
+                    )
+            else:
+                g = k - 8
+                t = ring.tile([P, 4, F2], BF16, name="raw", tag="ring")
+                nc.sync.dma_start(
+                    out=t[:],
+                    in_=fc2_kernel[g * 512 : (g + 1) * 512, :].rearrange("(p j) n -> p j n", j=4),
+                )
+            raw[k] = t
+            done["load"] = k + 1
+
+        def refill():
+            while done["load"] < 16:
+                freed = done["free"]
+                for k in range(done["load"]):
+                    if min(jobs_done("S"), jobs_done("V")) > last_use[k]:
+                        freed = freed + 1
+                if done["load"] + 4 - freed >= RING:
+                    break
+                load(done["load"])
+
+        for k in range(RING - 4):
+            load(k)
+        b2 = const.tile([P, F2], BF16, name="b2")
+        nc.sync.dma_start(out=b2[:], in_=fc2_bias.partition_broadcast(P))
+
+        grp = {}
+        wc = {}
+        ws = {}
+
+        def seg_src(job, si):
+            k, sub = job["segs"][si]
+            if job["kind"] == 1:
+                return raw[k][:, 4 * sub : 4 * sub + 4, :]
+            return raw[k][:, :, job["c0"] : job["c0"] + job["width"]]
+
+        def piece_list(is_vector):
+            pieces = []
+            for r, job in enumerate(jobs):
+                width = job["width"]
+                cut = CUTS["V" if is_vector else "S"].get(r, 0)
+                lo = 0 if is_vector else XS[r]
+                hi = XS[r] if is_vector else JW
+                for si in range(len(job["segs"])):
+                    a = max(lo, width * si)
+                    b = min(hi, width * (si + 1))
+                    while a < b:
+                        e = min(b, a + cut) if cut > 0 else b
+                        pieces.append((r, si, a, e))
+                        a = e
+            return pieces
+
+        todo = {"S": piece_list(False), "V": piece_list(True)}
+        copy_of = {"S": nc.scalar.copy, "V": nc.vector.tensor_copy}
+
+        def jobs_done(eng):
+            if done[eng] < len(todo[eng]):
+                return todo[eng][done[eng]][0]
+            return n_jobs
+
+        def emit(eng):
+            r, si, a, b = todo[eng][done[eng]]
+            done[eng] = done[eng] + 1
+            job = jobs[r]
+            width = job["width"]
+            if r not in grp:
+                grp[r] = grpp.tile([P, JW, 4], BF16, name="grp", tag="grp", align_bytes=64)
+            if job["kind"] == 1:
+                m0 = (a - width * si) // 4
+                m1 = (b - width * si) // 4
+                dst = grp[r][:, width * si : width * (si + 1), :].rearrange("p (t m) j -> p t m j", t=4)
+                src = seg_src(job, si).rearrange("p j (m t) -> p t m j", t=4)
+                copy_of[eng](out=dst[:, :, m0:m1, :], in_=src[:, :, m0:m1, :])
+            else:
+                regroup_part(
+                    copy_of[eng], grp[r][:, a:b, :],
+                    seg_src(job, si)[:, :, a - width * si : b - width * si],
+                )
+
+        def run_seq(eng, tokens):
+            for ch in tokens:
+                if ch == "p":
+                    if done[eng] < len(todo[eng]):
+                        emit(eng)
+                else:
+                    w_quant(done["quant"])
+
+        def regroup_upto(eng, j):
+            while jobs_done(eng) < min(j, n_jobs):
+                emit(eng)
+
+        def w_quant(r):
+            regroup_upto("V", r + 1)
+            regroup_upto("S", r + 1)
+            width = jobs[r]["width"]
+            wc[r] = codp.tile([P, JW], U32, name="wc", tag="wc", align_bytes=64)
+            ws[r] = codp.tile([P, JW], U8, name="ws", tag="ws", align_bytes=64)
+            for s0, s1 in QSPLIT.get(r, [(0, len(jobs[r]["segs"]))]):
+                a = s0 * width
+                b = s1 * width
+                quantise(wc[r][:, a:b], ws[r][:, a:b], grp[r][:, a:b, :], b - a)
+            done["quant"] = r + 1
+
+        slot = {0: 0, 2: 1, 3: 2, 1: 3}
+        junk = const.tile([P, D], BF16, name="junk")
+        sum1 = const.tile([P, 1], F32, name="sum1")
+        negmu1 = const.tile([P, 1], F32, name="negmu1")
+        ssq1 = const.tile([P, 1], F32, name="ssq1")
+        nc.scalar.activation(out=junk[:], in_=x_all[:, 1, :], func=ACT.Identity, accum_out=sum1[:])
+        nc.scalar.mul(out=negmu1[:], in_=sum1[:], mul=-1.0 / D)
+        nc.scalar.activation(
+            out=junk[:], in_=x_all[:, 1, :], func=ACT.Square, bias=negmu1[:, 0:1], scale=1.0,
+            accum_out=ssq1[:],
+        )
+
+        stats = const.tile([P, 3, 2, 6], F32, name="stats")
+        mv = const.tile([P, 3, 2], F32, name="mv")
+        vt_ps = psum.tile([P, 4, P], BF16, name="vt_ps", tag="bank0")
+        for t in range(4):
+            nc.tensor.transpose(vt_ps[:, t, :], vec[:, t::4], ident_b[:])
+        vec_t = const.tile([P, 4, 12], F32, name="vec_t")
+        for i in (0, 2, 3):
+            for s in range(2):
+                nc.vector.bn_stats(
+                    out=stats[:, slot[i], s, :], in_=x_all[:, i, s * 512 : (s + 1) * 512]
+                )
+            nc.vector.bn_aggr(
+                out=mv[:, slot[i], :], in_=stats[:, slot[i], :, :].rearrange("p s k -> p (s k)")
+            )
+            if i == 0:
+                nc.vector.tensor_copy(out=vec_t[:], in_=vt_ps[:, :, 0:12])
+
+        negmean = const.tile([P, 4], F32, name="negmean")
+        nc.vector.tensor_scalar(
+            out=negmean[:, 0:3], in0=mv[:, :, 0], scalar1=-1.0, scalar2=None, op0=ALU.mult
+        )
+        nc.vector.tensor_copy(out=negmean[:, 3:4], in_=negmu1[:])
+        run_seq("S", S_SEQ[0])
+        std = const.tile([P, 4], F32, name="std")
+        nc.scalar.activation(
+            out=std[:, 3:4], in_=ssq1[:], func=ACT.Sqrt, bias=eps_t[:, 0:1], scale=1.0 / D
+        )
+        nc.scalar.activation(
+            out=std[:, 0:3], in_=mv[:, :, 1], func=ACT.Sqrt, bias=eps_t[:, 0:1], scale=1.0
+        )
+        run_seq("V", V_SEQ[0])
+        rstd = const.tile([P, 4], F32, name="rstd")
+        nc.vector.reciprocal(out=rstd[:], in_=std[:])
+        nmr = const.tile([P, 4], F32, name="nmr")
+        nc.vector.tensor_tensor(out=nmr[:], in0=negmean[:], in1=rstd[:], op=ALU.mult)
+        run_seq("S", S_SEQ[1])
+
+        ln_ps = []
+        for b in range(8):
+            ln_b = psum.tile([P, T], F32, name="ln_ps%d" % b, tag="bank%d" % b)
+            ln_ps.append(ln_b)
+        xh = []
+        for half in range(2):
+            xh_h = ring.tile([P, 2, D], F32, name="xh", tag="ring")
+            xh.append(xh_h)
+        for i in range(4):
+            xh_i = xh[i // 2][:, i % 2, :]
+            xh_v = xh_i.rearrange("q (c t p) -> q c t p", c=2, t=4)
+            x_v = x_all[:, i, :].rearrange("q (c p t) -> q c t p", c=2, t=4)
+            s = slot[i]
+            if XH_ON[i] == "S":
+                nc.scalar.activation(
+                    out=xh_v, in_=x_v, func=ACT.Identity,
+                    scale=rstd[:, s : s + 1], bias=nmr[:, s : s + 1],
+                )
+            else:
+                nc.vector.tensor_scalar(
+                    out=xh_v, in0=x_v, scalar1=negmean[:, s : s + 1],
+                    scalar2=rstd[:, s : s + 1], op0=ALU.add, op1=ALU.mult,
+                )
+            for b in range(8):
+                nc.tensor.transpose(
+                    ln_ps[b][:, i * P : (i + 1) * P], xh_i[:, b * P : (b + 1) * P], ident_f[:]
+                )
+        lnp = ring.tile([P, 8, T], BF16, name="lnp", tag="ring")
+        done["free"] = 3
+        refill()
+        nc.scalar.activation(out=warm[:, 1:2], in_=std[:, 0:1], func=ACT.Gelu_apprx_tanh)
+        run_seq("S", S_SEQ[2])
+        run_seq("V", V_SEQ[1])
+        refill()
+
+        for b in EV_ORDER:
+            if EV_ON[b] == "S":
+                nc.scalar.activation(
+                    out=lnp[:, b, :], in_=ln_ps[b][:], func=ACT.Identity,
+                    scale=vec_t[:, b % 4, b // 4 : b // 4 + 1],
+                    bias=vec_t[:, b % 4, 2 + b // 4 : 3 + b // 4],
+                )
+            else:
+                nc.vector.tensor_scalar(
+                    out=lnp[:, b, :], in0=ln_ps[b][:],
+                    scalar1=vec_t[:, b % 4, b // 4 : b // 4 + 1],
+                    scalar2=vec_t[:, b % 4, 2 + b // 4 : 3 + b // 4], op0=ALU.mult, op1=ALU.add,
+                )
+        lnc = const.tile([P, 2 * T], U32, name="lnc", align_bytes=64)
+        lns = const.tile([P, 2 * T], U8, name="lns", align_bytes=64)
+        lng = grpp.tile([P, JW, 4], BF16, name="grp", tag="grp", align_bytes=64)
+        for g in range(2):
+            regroup_part(
+                nc.vector.tensor_copy, lng[:, g * T : (g + 1) * T, :], lnp[:, 4 * g : 4 * g + 4, :]
+            )
+        done["free"] = 4
+        refill()
+        run_seq("V", V_SEQ[2])
+        refill()
+        quantise(lnc[:], lns[:], lng[:], 2 * T)
+
+        hc = const.tile([P, 8 * T], U32, name="hc", align_bytes=64)
+        hs = const.tile([P, 8 * T], U8, name="hs", align_bytes=64)
+        acc1 = {}
+        acc2 = {}
+        hp = {}
+        hg = {}
+
+        def fc1(q):
+            for j in range(4):
+                acc = psum.tile([P, T], F32, name="acc1", tag="bank%d" % ((4 * q + j) % 8))
+                for c in range(2):
+                    a = c * 512 + j * P
+                    nc.tensor.matmul_mx(
+                        out=acc[:],
+                        lhsT=wc[q][:, a : a + P].bitcast(FP8X4),
+                        lhsT_scale=ws[q][:, a : a + P],
+                        rhs=lnc[:, c * T : (c + 1) * T].bitcast(FP8X4),
+                        rhs_scale=lns[:, c * T : (c + 1) * T],
+                        start=(c == 0),
+                        stop=(c == 1),
+                    )
+                acc1[(q, j)] = acc
+
+        def gelu(q):
+            hp[q] = hpp.tile([P, 4, T], BF16, name="hp", tag="hp")
+            for j in range(4):
+                nc.scalar.activation(
+                    out=hp[q][:, j, :], in_=acc1[(q, j)][:], func=ACT.Gelu_apprx_tanh,
+                    bias=vec_t[:, j, 4 + q : 5 + q], scale=1.0,
+                )
+
+        def h_regroup(q):
+            if q % 2 == 0:
+                hg[q // 2] = hgp.tile([P, JW, 4], BF16, name="hg", tag="hg", align_bytes=64)
+            regroup_part(
+                nc.vector.tensor_copy, hg[q // 2][:, (q % 2) * T : (q % 2 + 1) * T, :], hp[q][:]
+            )
+
+        def h_quant(q):
+            if q % 2 == 1:
+                a = (q - 1) * T
+                quantise(hc[:, a : a + 2 * T], hs[:, a : a + 2 * T], hg[q // 2][:], 2 * T)
+
+        def fc2(r):
+            job = jobs[r]
+            width = job["width"]
+            bi = job["block"]
+            for si in range(len(job["segs"])):
+                g = job["segs"][si][1]
+                for i in range(4):
+                    if g == 0:
+                        acc2[(bi, i)] = psum.tile(
+                            [P, width], F32, name="acc2", tag="bank%d" % (4 * (bi % 2) + i)
+                        )
+                    a = g * T + i * P
+                    nc.tensor.matmul_mx(
+                        out=acc2[(bi, i)][:],
+                        lhsT=hc[:, a : a + P].bitcast(FP8X4),
+                        lhsT_scale=hs[:, a : a + P],
+                        rhs=wc[r][:, si * width : (si + 1) * width].bitcast(FP8X4),
+                        rhs_scale=ws[r][:, si * width : (si + 1) * width],
+                        start=(g == 0),
+                        stop=(g == 7),
+                    )
+
+        def finish(bi):
+            c0, width = BLOCKS[bi]
+            for i in range(4):
+                o_sb = outp.tile([P, width], F32, name="o_sb", tag="o_sb")
+                nc.vector.tensor_tensor(
+                    out=o_sb[:], in0=acc2[(bi, i)][:], in1=b2[:, c0 : c0 + width], op=ALU.add
+                )
+                nc.sync.dma_start(out=out[i * P : (i + 1) * P, c0 : c0 + width], in_=o_sb[:])
+
+        fin_at = {}
+        for ji, job in enumerate(jobs):
+            if job["kind"] == 2:
+                fin_at[job["block"]] = ji + FIN_DELAY
+
+        for r in range(n_jobs):
+            regroup_upto("S", r + 1 + LOOK_S)
+            regroup_upto("V", r + 1 + LOOK_V)
+            refill()
+            if 0 <= r - DG < 8:
+                gelu(r - DG)
+            if 0 <= r - DH < 8:
+                h_regroup(r - DH)
+            if r >= done["quant"]:
+                w_quant(r)
+            if 0 <= r - DH < 8:
+                h_quant(r - DH)
+            if r < 8:
+                fc1(r)
+            else:
+                fc2(r)
+            for bi in range(len(BLOCKS)):
+                if fin_at[bi] == r:
+                    finish(bi)
+        for bi in range(len(BLOCKS)):
+            if fin_at[bi] >= n_jobs:
+                finish(bi)

@@ -99,6 +99,7 @@ def tile_layernormmlp_kernel(
         nc.vector.memset(eps_t[:], EPS)
         vec = const.tile([P, 512], BF16, name="vec")
         nc.vector.memset(vec[:], 0.0)
+        vec_h = const.tile([P, 512], BF16, name="vec_h")
 
         x_all = ring.tile([P, 4, D], BF16, name="x_all", tag="ring")
         for i in range(4):
@@ -125,10 +126,9 @@ def tile_layernormmlp_kernel(
             else:
                 g = k - 8
                 t = ring.tile([P, 4, F2], BF16, name="raw", tag="ring")
-                nc.sync.dma_start(
-                    out=t[:],
-                    in_=fc2_kernel[g * 512 : (g + 1) * 512, :].rearrange("(p j) n -> p j n", j=4),
-                )
+                rows = fc2_kernel[g * 512 : (g + 1) * 512, :].rearrange("(x j e) n -> e x j n", j=4, e=4)
+                for e in range(4):
+                    nc.sync.dma_start(out=t[e::4, :, :], in_=rows[e])
             raw[k] = t
             done["load"] = k + 1
 
@@ -189,11 +189,13 @@ def tile_layernormmlp_kernel(
             if r not in grp:
                 grp[r] = grpp.tile([P, JW, 4], BF16, name="grp", tag="grp", align_bytes=64)
             if job["kind"] == 1:
-                m0 = (a - width * si) // 4
-                m1 = (b - width * si) // 4
-                dst = grp[r][:, width * si : width * (si + 1), :].rearrange("p (t m) j -> p t m j", t=4)
-                src = seg_src(job, si).rearrange("p j (m t) -> p t m j", t=4)
-                copy_of[eng](out=dst[:, :, m0:m1, :], in_=src[:, :, m0:m1, :])
+                x0 = (a - width * si) // 16
+                x1 = (b - width * si) // 16
+                dst = grp[r][:, width * si : width * (si + 1), :].rearrange(
+                    "p (t x e) j -> p t x j e", t=4, e=4
+                )
+                src = seg_src(job, si).rearrange("p j (x t e) -> p t x j e", t=4, e=4)
+                copy_of[eng](out=dst[:, :, x0:x1], in_=src[:, :, x0:x1])
             else:
                 regroup_part(
                     copy_of[eng], grp[r][:, a:b, :],
@@ -238,10 +240,16 @@ def tile_layernormmlp_kernel(
 
         stats = const.tile([P, 3, 2, 6], F32, name="stats")
         mv = const.tile([P, 3, 2], F32, name="mv")
-        vt_ps = psum.tile([P, 4, P], BF16, name="vt_ps", tag="bank0")
+        nc.vector.tensor_copy(
+            out=vec_h[:].rearrange("r (t x e) -> r t x e", t=4, e=4),
+            in_=vec[:].rearrange("r (x t e) -> r t x e", t=4, e=4),
+        )
+        vt_ps = psum.tile([P, 8, P], BF16, name="vt_ps", tag="bank0")
         for t in range(4):
             nc.tensor.transpose(vt_ps[:, t, :], vec[:, t::4], ident_b[:])
-        vec_t = const.tile([P, 4, 12], F32, name="vec_t")
+        for t in range(4):
+            nc.tensor.transpose(vt_ps[:, 4 + t, :], vec_h[:, t * P : (t + 1) * P], ident_b[:])
+        vec_t = const.tile([P, 8, 12], F32, name="vec_t")
         for i in (0, 2, 3):
             for s in range(2):
                 nc.vector.bn_stats(
@@ -362,7 +370,7 @@ def tile_layernormmlp_kernel(
             for j in range(4):
                 nc.scalar.activation(
                     out=hp[q][:, j, :], in_=acc1[(q, j)][:], func=ACT.Gelu_apprx_tanh,
-                    bias=vec_t[:, j, 4 + q : 5 + q], scale=1.0,
+                    bias=vec_t[:, 4 + j, 4 + q : 5 + q], scale=1.0,
                 )
 
         def h_regroup(q):

@@ -141,11 +141,12 @@ def tile_layernormmlp_kernel(
                 if done["load"] + 4 - freed >= RING:
                     break
                 load(done["load"])
+                if done["load"] == 16:
+                    nc.sync.dma_start(out=b2[:], in_=fc2_bias.partition_broadcast(P))
 
         for k in range(RING - 4):
             load(k)
         b2 = const.tile([P, F2], BF16, name="b2")
-        nc.sync.dma_start(out=b2[:], in_=fc2_bias.partition_broadcast(P))
 
         grp = {}
         wc = {}
@@ -240,15 +241,9 @@ def tile_layernormmlp_kernel(
 
         stats = const.tile([P, 3, 2, 6], F32, name="stats")
         mv = const.tile([P, 3, 2], F32, name="mv")
-        nc.vector.tensor_copy(
-            out=vec_h[:].rearrange("r (t x e) -> r t x e", t=4, e=4),
-            in_=vec[:].rearrange("r (x t e) -> r t x e", t=4, e=4),
-        )
         vt_ps = psum.tile([P, 8, P], BF16, name="vt_ps", tag="bank0")
         for t in range(4):
             nc.tensor.transpose(vt_ps[:, t, :], vec[:, t::4], ident_b[:])
-        for t in range(4):
-            nc.tensor.transpose(vt_ps[:, 4 + t, :], vec_h[:, t * P : (t + 1) * P], ident_b[:])
         vec_t = const.tile([P, 8, 12], F32, name="vec_t")
         for i in (0, 2, 3):
             for s in range(2):
@@ -258,14 +253,18 @@ def tile_layernormmlp_kernel(
             nc.vector.bn_aggr(
                 out=mv[:, slot[i], :], in_=stats[:, slot[i], :, :].rearrange("p s k -> p (s k)")
             )
-            if i == 0:
-                nc.vector.tensor_copy(out=vec_t[:], in_=vt_ps[:, :, 0:12])
 
         negmean = const.tile([P, 4], F32, name="negmean")
         nc.vector.tensor_scalar(
             out=negmean[:, 0:3], in0=mv[:, :, 0], scalar1=-1.0, scalar2=None, op0=ALU.mult
         )
         nc.vector.tensor_copy(out=negmean[:, 3:4], in_=negmu1[:])
+        nc.vector.tensor_copy(
+            out=vec_h[:].rearrange("r (t x e) -> r t x e", t=4, e=4),
+            in_=vec[:].rearrange("r (x t e) -> r t x e", t=4, e=4),
+        )
+        for t in range(4):
+            nc.tensor.transpose(vt_ps[:, 4 + t, :], vec_h[:, t * P : (t + 1) * P], ident_b[:])
         run_seq("S", S_SEQ[0])
         std = const.tile([P, 4], F32, name="std")
         nc.scalar.activation(
@@ -279,6 +278,7 @@ def tile_layernormmlp_kernel(
         nc.vector.reciprocal(out=rstd[:], in_=std[:])
         nmr = const.tile([P, 4], F32, name="nmr")
         nc.vector.tensor_tensor(out=nmr[:], in0=negmean[:], in1=rstd[:], op=ALU.mult)
+        nc.vector.tensor_copy(out=vec_t[:], in_=vt_ps[:, :, 0:12])
         run_seq("S", S_SEQ[1])
 
         ln_ps = []

@@ -22,22 +22,21 @@ FLOPS = 2 * T * D * F1 + 2 * T * F1 * F2
 JW = 1024
 RING = 12
 BLOCKS = [[0,512],[512,256],[768,256]]
-XS = [1008,912,384,560,1024,1024,752,544,368,400,400,112,384,272,304,0]
-QSPLIT = {15: [[0,2],[2,3],[3,4]]}
+XS = [768,640,384,560,1024,1024,752,544,368,400,400,112,384,272,304,0]
+QSPLIT = {15: [[0,1],[1,2],[2,3],[3,4]]}
 LOOK_S = 1
 LOOK_V = 1
 DG = 2
 DH = 3
-XH_ON = "SSSS"
 EV_ON = "SSVVSSVV"
 EV_ORDER = [0,2,1,3,4,6,5,7]
-V_SEQ = ["p","ppppqpp","q"]
-S_SEQ = ["p","","p"]
+V_SEQ = ["p","ppppp","q"]
+S_SEQ = ["","",""]
 CUTS = {"V": {0: 256}, "S": {0: 256}}
 COD_BUFS = 4
 Q_COLS = 512
 GRP_BUFS = 5
-FIN_DELAY = 1
+FIN_DELAY = [1, 2, 1]
 PINNED = True
 
 
@@ -72,7 +71,7 @@ def tile_layernormmlp_kernel(
         codp = ctx.enter_context(tc.tile_pool(name="codp", bufs=COD_BUFS))
         hpp = ctx.enter_context(tc.tile_pool(name="hpp", bufs=3))
         hgp = ctx.enter_context(tc.tile_pool(name="hgp", bufs=2))
-        outp = ctx.enter_context(tc.tile_pool(name="outp", bufs=4))
+        outp = ctx.enter_context(tc.tile_pool(name="outp", bufs=8))
         psum = ctx.enter_context(tc.psum_pool(name="psum", bufs=1))
         if PINNED:
             ctx.enter_context(tc.manual_schedule())
@@ -227,7 +226,10 @@ def tile_layernormmlp_kernel(
                 quantise(wc[r][:, a:b], ws[r][:, a:b], grp[r][:, a:b, :], b - a)
             done["quant"] = r + 1
 
-        slot = {0: 0, 2: 1, 3: 2, 1: 3}
+        slot = {0: 0, 2: 1, 1: 2, 3: 3}
+        rstd = const.tile([P, 4], F32, name="rstd")
+        nmr = const.tile([P, 4], F32, name="nmr")
+        nmr1 = const.tile([P, 1], F32, name="nmr1")
         junk = const.tile([P, D], BF16, name="junk")
         sum1 = const.tile([P, 1], F32, name="sum1")
         negmu1 = const.tile([P, 1], F32, name="negmu1")
@@ -239,47 +241,58 @@ def tile_layernormmlp_kernel(
             accum_out=ssq1[:],
         )
 
-        stats = const.tile([P, 3, 2, 6], F32, name="stats")
-        mv = const.tile([P, 3, 2], F32, name="mv")
+        stats = const.tile([P, 4, 2, 6], F32, name="stats")
+        mv = const.tile([P, 4, 2], F32, name="mv")
         vt_ps = psum.tile([P, 8, P], BF16, name="vt_ps", tag="bank0")
         for t in range(4):
             nc.tensor.transpose(vt_ps[:, t, :], vec[:, t::4], ident_b[:])
         vec_t = const.tile([P, 8, 12], F32, name="vec_t")
-        for i in (0, 2, 3):
-            for s in range(2):
-                nc.vector.bn_stats(
-                    out=stats[:, slot[i], s, :], in_=x_all[:, i, s * 512 : (s + 1) * 512]
-                )
+
+        def bn(i, h):
+            nc.vector.bn_stats(
+                out=stats[:, slot[i], h, :], in_=x_all[:, i, h * 512 : (h + 1) * 512]
+            )
+
+        def aggr(i):
             nc.vector.bn_aggr(
                 out=mv[:, slot[i], :], in_=stats[:, slot[i], :, :].rearrange("p s k -> p (s k)")
             )
 
-        negmean = const.tile([P, 4], F32, name="negmean")
-        nc.vector.tensor_scalar(
-            out=negmean[:, 0:3], in0=mv[:, :, 0], scalar1=-1.0, scalar2=None, op0=ALU.mult
+        std = const.tile([P, 4], F32, name="std")
+
+        def rs_of(a, b):
+            nc.scalar.activation(
+                out=std[:, a:b], in_=mv[:, a:b, 1], func=ACT.Sqrt, bias=eps_t[:, 0:1], scale=1.0,
+            )
+
+        def nmr_of(a, b):
+            nc.vector.scalar_tensor_tensor(
+                out=nmr[:, a:b], in0=mv[:, a:b, 0], scalar=-1.0, in1=rstd[:, a:b],
+                op0=ALU.mult, op1=ALU.mult,
+            )
+
+        bn(0, 0)
+        bn(0, 1)
+        bn(2, 0)
+        aggr(0)
+        bn(2, 1)
+        bn(3, 0)
+        aggr(2)
+        nc.scalar.activation(
+            out=std[:, 2:3], in_=ssq1[:], func=ACT.Sqrt, bias=eps_t[:, 0:1], scale=1.0 / D
         )
-        nc.vector.tensor_copy(out=negmean[:, 3:4], in_=negmu1[:])
+        rs_of(0, 2)
+        bn(3, 1)
+        nc.vector.reciprocal(out=rstd[:, 0:3], in_=std[:, 0:3])
+        nc.scalar.mul(out=nmr1[:], in_=negmu1[:], mul=rstd[:, 2:3])
+        nmr_of(0, 2)
+        aggr(3)
         nc.vector.tensor_copy(
             out=vec_h[:].rearrange("r (t x e) -> r t x e", t=4, e=4),
             in_=vec[:].rearrange("r (x t e) -> r t x e", t=4, e=4),
         )
         for t in range(4):
             nc.tensor.transpose(vt_ps[:, 4 + t, :], vec_h[:, t * P : (t + 1) * P], ident_b[:])
-        run_seq("S", S_SEQ[0])
-        std = const.tile([P, 4], F32, name="std")
-        nc.scalar.activation(
-            out=std[:, 3:4], in_=ssq1[:], func=ACT.Sqrt, bias=eps_t[:, 0:1], scale=1.0 / D
-        )
-        nc.scalar.activation(
-            out=std[:, 0:3], in_=mv[:, :, 1], func=ACT.Sqrt, bias=eps_t[:, 0:1], scale=1.0
-        )
-        run_seq("V", V_SEQ[0])
-        rstd = const.tile([P, 4], F32, name="rstd")
-        nc.vector.reciprocal(out=rstd[:], in_=std[:])
-        nmr = const.tile([P, 4], F32, name="nmr")
-        nc.vector.tensor_tensor(out=nmr[:], in0=negmean[:], in1=rstd[:], op=ALU.mult)
-        nc.vector.tensor_copy(out=vec_t[:], in_=vt_ps[:, :, 0:12])
-        run_seq("S", S_SEQ[1])
 
         ln_ps = []
         for b in range(8):
@@ -289,25 +302,25 @@ def tile_layernormmlp_kernel(
         for half in range(2):
             xh_h = ring.tile([P, 2, D], F32, name="xh", tag="ring")
             xh.append(xh_h)
-        for i in range(4):
+        for i in (1, 0, 2, 3):
             xh_i = xh[i // 2][:, i % 2, :]
-            xh_v = xh_i.rearrange("q (c t p) -> q c t p", c=2, t=4)
-            x_v = x_all[:, i, :].rearrange("q (c p t) -> q c t p", c=2, t=4)
-            s = slot[i]
-            if XH_ON[i] == "S":
-                nc.scalar.activation(
-                    out=xh_v, in_=x_v, func=ACT.Identity,
-                    scale=rstd[:, s : s + 1], bias=nmr[:, s : s + 1],
-                )
-            else:
-                nc.vector.tensor_scalar(
-                    out=xh_v, in0=x_v, scalar1=negmean[:, s : s + 1],
-                    scalar2=rstd[:, s : s + 1], op0=ALU.add, op1=ALU.mult,
-                )
+            sc = rstd[:, slot[i] : slot[i] + 1]
+            sh = nmr1[:, 0:1] if i == 1 else nmr[:, slot[i] : slot[i] + 1]
+            nc.scalar.activation(
+                out=xh_i.rearrange("q (c t p) -> q c t p", c=2, t=4),
+                in_=x_all[:, i, :].rearrange("q (c p t) -> q c t p", c=2, t=4),
+                func=ACT.Identity, scale=sc, bias=sh,
+            )
             for b in range(8):
                 nc.tensor.transpose(
                     ln_ps[b][:, i * P : (i + 1) * P], xh_i[:, b * P : (b + 1) * P], ident_f[:]
                 )
+            if i == 1:
+                rs_of(3, 4)
+                run_seq("V", V_SEQ[0])
+                nc.vector.reciprocal(out=rstd[:, 3:4], in_=std[:, 3:4])
+                nmr_of(3, 4)
+                nc.vector.tensor_copy(out=vec_t[:], in_=vt_ps[:, :, 0:12])
         lnp = ring.tile([P, 8, T], BF16, name="lnp", tag="ring")
         done["free"] = 3
         refill()
@@ -419,7 +432,7 @@ def tile_layernormmlp_kernel(
         fin_at = {}
         for ji, job in enumerate(jobs):
             if job["kind"] == 2:
-                fin_at[job["block"]] = ji + FIN_DELAY
+                fin_at[job["block"]] = ji + FIN_DELAY[job["block"]]
 
         for r in range(n_jobs):
             regroup_upto("S", r + 1 + LOOK_S)

@@ -22,7 +22,7 @@ FLOPS = 2 * T * D * F1 + 2 * T * F1 * F2
 JW = 1024
 RING = 12
 BLOCKS = [[0,512],[512,256],[768,256]]
-XS = [768,640,384,560,1024,1024,752,544,368,400,400,112,384,272,304,0]
+XS = [768, 768, 384, 768, 576, 576, 576, 576, 576, 576, 576, 256, 384, 256, 384, 256]
 QSPLIT = {15: [[0,1],[1,2],[2,3],[3,4]]}
 LOOK_S = 1
 LOOK_V = 1

@@ -22,7 +22,7 @@ FLOPS = 2 * T * D * F1 + 2 * T * F1 * F2
 JW = 1024
 RING = 12
 BLOCKS = [[0,512],[512,256],[768,256]]
-XS = [768, 768, 384, 768, 576, 576, 576, 576, 576, 576, 576, 256, 384, 256, 384, 256]
+XS = [768, 768, 384, 768, 576, 576, 576, 576, 576, 576, 576, 384, 384, 384, 384, 384]
 QSPLIT = {15: [[0,1],[1,2],[2,3],[3,4]]}
 LOOK_S = 1
 LOOK_V = 1
@@ -30,13 +30,14 @@ DG = 2
 DH = 3
 EV_ON = "SSVVSSVV"
 EV_ORDER = [0,2,1,3,4,6,5,7]
-V_SEQ = ["p","ppppp","q"]
+V_SEQ = ["pp","pppp","q"]
 S_SEQ = ["","",""]
 CUTS = {"V": {0: 256}, "S": {0: 256}}
 COD_BUFS = 4
 Q_COLS = 512
 GRP_BUFS = 5
-FIN_DELAY = [1, 2, 1]
+FIN_BEFORE = {}
+FIN_AFTER = {14: [[1, 0, 4]], 15: [[0, 0, 4]]}
 PINNED = True
 
 
@@ -243,7 +244,7 @@ def tile_layernormmlp_kernel(
 
         stats = const.tile([P, 4, 2, 6], F32, name="stats")
         mv = const.tile([P, 4, 2], F32, name="mv")
-        vt_ps = psum.tile([P, 8, P], BF16, name="vt_ps", tag="bank0")
+        vt_ps = psum.tile([P, 8, P], BF16, name="vt_ps", tag="bank7")
         for t in range(4):
             nc.tensor.transpose(vt_ps[:, t, :], vec[:, t::4], ident_b[:])
         vec_t = const.tile([P, 8, 12], F32, name="vec_t")
@@ -318,9 +319,9 @@ def tile_layernormmlp_kernel(
             if i == 1:
                 rs_of(3, 4)
                 run_seq("V", V_SEQ[0])
+                nc.vector.tensor_copy(out=vec_t[:], in_=vt_ps[:, :, 0:12])
                 nc.vector.reciprocal(out=rstd[:, 3:4], in_=std[:, 3:4])
                 nmr_of(3, 4)
-                nc.vector.tensor_copy(out=vec_t[:], in_=vt_ps[:, :, 0:12])
         lnp = ring.tile([P, 8, T], BF16, name="lnp", tag="ring")
         done["free"] = 3
         refill()
@@ -407,7 +408,7 @@ def tile_layernormmlp_kernel(
                 for i in range(4):
                     if g == 0:
                         acc2[(bi, i)] = psum.tile(
-                            [P, width], F32, name="acc2", tag="bank%d" % (4 * (bi % 2) + i)
+                            [P, width], F32, name="acc2", tag="bank%d" % (4 * min(bi, 1) + i)
                         )
                     a = g * T + i * P
                     nc.tensor.matmul_mx(
@@ -420,19 +421,14 @@ def tile_layernormmlp_kernel(
                         stop=(g == 7),
                     )
 
-        def finish(bi):
+        def finish(bi, i0, i1):
             c0, width = BLOCKS[bi]
-            for i in range(4):
+            for i in range(i0, i1):
                 o_sb = outp.tile([P, width], F32, name="o_sb", tag="o_sb")
                 nc.vector.tensor_tensor(
                     out=o_sb[:], in0=acc2[(bi, i)][:], in1=b2[:, c0 : c0 + width], op=ALU.add
                 )
                 nc.sync.dma_start(out=out[i * P : (i + 1) * P, c0 : c0 + width], in_=o_sb[:])
-
-        fin_at = {}
-        for ji, job in enumerate(jobs):
-            if job["kind"] == 2:
-                fin_at[job["block"]] = ji + FIN_DELAY[job["block"]]
 
         for r in range(n_jobs):
             regroup_upto("S", r + 1 + LOOK_S)
@@ -442,17 +438,16 @@ def tile_layernormmlp_kernel(
                 gelu(r - DG)
             if 0 <= r - DH < 8:
                 h_regroup(r - DH)
+            for bi, i0, i1 in FIN_BEFORE.get(r, []):
+                finish(bi, i0, i1)
             if r >= done["quant"]:
                 w_quant(r)
             if 0 <= r - DH < 8:
                 h_quant(r - DH)
+            for bi, i0, i1 in FIN_AFTER.get(r, []):
+                finish(bi, i0, i1)
             if r < 8:
                 fc1(r)
             else:
                 fc2(r)
-            for bi in range(len(BLOCKS)):
-                if fin_at[bi] == r:
-                    finish(bi)
-        for bi in range(len(BLOCKS)):
-            if fin_at[bi] >= n_jobs:
-                finish(bi)
+        finish(2, 0, 4)

@@ -22,11 +22,13 @@ FLOPS = 2 * T * D * F1 + 2 * T * F1 * F2
 JW = 1024
 RING = 12
 BLOCKS = [[0,512],[512,256],[768,256]]
-XS = [768, 768, 384, 768, 576, 576, 576, 576, 576, 576, 576, 384, 384, 384, 384, 384]
+XS = [640,640,384,640,544,544,544,544,544,544,544,384,384,384,384,384]
 QSPLIT = {15: [[0,1],[1,2],[2,3],[3,4]]}
 LOOK_S = 1
+PE_JOBS = [1, 2, 3, 4, 5, 6, 7]
+STAGED = 768
 LOOK_V = 1
-DG = 2
+DG = 1
 DH = 3
 EV_ON = "SSVVSSVV"
 EV_ORDER = [0,2,1,3,4,6,5,7]
@@ -111,7 +113,7 @@ def tile_layernormmlp_kernel(
         nc.scalar.activation(out=warm[:, 0:1], in_=eps_t[:], func=ACT.Sqrt)
 
         raw = {}
-        done = {"S": 0, "V": 0, "load": 0, "free": 0, "quant": 0}
+        done = {"S": 0, "V": 0, "load": 0, "free": 0, "quant": 0, "staged": 0}
 
         def load(k):
             if k < 8:
@@ -164,7 +166,7 @@ def tile_layernormmlp_kernel(
                 width = job["width"]
                 cut = CUTS["V" if is_vector else "S"].get(r, 0)
                 lo = 0 if is_vector else XS[r]
-                hi = XS[r] if is_vector else JW
+                hi = XS[r] if is_vector else (STAGED if r in PE_JOBS else JW)
                 for si in range(len(job["segs"])):
                     a = max(lo, width * si)
                     b = min(hi, width * (si + 1))
@@ -172,6 +174,8 @@ def tile_layernormmlp_kernel(
                         e = min(b, a + cut) if cut > 0 else b
                         pieces.append((r, si, a, e))
                         a = e
+                if not is_vector and r in PE_JOBS:
+                    pieces.append((r, 1, STAGED, JW))
             return pieces
 
         todo = {"S": piece_list(False), "V": piece_list(True)}
@@ -189,7 +193,13 @@ def tile_layernormmlp_kernel(
             width = job["width"]
             if r not in grp:
                 grp[r] = grpp.tile([P, JW, 4], BF16, name="grp", tag="grp", align_bytes=64)
-            if job["kind"] == 1:
+            if eng == "S" and r in PE_JOBS and a == STAGED:
+                st = stage.pop(r)
+                nc.scalar.copy(
+                    out=grp[r][:, 512:JW, :].rearrange("p (t w) j -> p t (w j)", t=4)[:, :, 256:512],
+                    in_=st[:].rearrange("p t w j -> p t (w j)"),
+                )
+            elif job["kind"] == 1:
                 x0 = (a - width * si) // 16
                 x1 = (b - width * si) // 16
                 dst = grp[r][:, width * si : width * (si + 1), :].rearrange(
@@ -202,6 +212,21 @@ def tile_layernormmlp_kernel(
                     copy_of[eng], grp[r][:, a:b, :],
                     seg_src(job, si)[:, :, a - width * si : b - width * si],
                 )
+
+        stage = {}
+
+        def stage_upto(j):
+            while done["staged"] < len(PE_JOBS) and PE_JOBS[done["staged"]] < j:
+                r = PE_JOBS[done["staged"]]
+                st = psum.tile([P, 4, 64, 4], BF16, name="st", tag="bank%d" % (done["staged"] % 2))
+                src = raw[r][:, 4:8, :].rearrange("p j (x t e) -> p t x e j", t=4, e=4)
+                for t in range(4):
+                    nc.tensor.matmul(
+                        out=st[:, t, :, :].rearrange("p (x e) j -> p x e j", e=4),
+                        lhsT=ident_b[:], rhs=src[:, t, 16:32], start=True, stop=True,
+                    )
+                stage[r] = st
+                done["staged"] = done["staged"] + 1
 
         def run_seq(eng, tokens):
             for ch in tokens:
@@ -343,6 +368,7 @@ def tile_layernormmlp_kernel(
                     scalar1=vec_t[:, b % 4, b // 4 : b // 4 + 1],
                     scalar2=vec_t[:, b % 4, 2 + b // 4 : 3 + b // 4], op0=ALU.mult, op1=ALU.add,
                 )
+        stage_upto(3)
         lnc = const.tile([P, 2 * T], U32, name="lnc", align_bytes=64)
         lns = const.tile([P, 2 * T], U8, name="lns", align_bytes=64)
         lng = grpp.tile([P, JW, 4], BF16, name="grp", tag="grp", align_bytes=64)
@@ -365,7 +391,7 @@ def tile_layernormmlp_kernel(
 
         def fc1(q):
             for j in range(4):
-                acc = psum.tile([P, T], F32, name="acc1", tag="bank%d" % ((4 * q + j) % 8))
+                acc = psum.tile([P, T], F32, name="acc1", tag="bank%d" % (2 + (4 * q + j) % 6))
                 for c in range(2):
                     a = c * 512 + j * P
                     nc.tensor.matmul_mx(
@@ -408,7 +434,7 @@ def tile_layernormmlp_kernel(
                 for i in range(4):
                     if g == 0:
                         acc2[(bi, i)] = psum.tile(
-                            [P, width], F32, name="acc2", tag="bank%d" % (4 * min(bi, 1) + i)
+                            [P, width], F32, name="acc2", tag="bank%d" % ((2 + 4 * min(bi, 1) + i) % 8)
                         )
                     a = g * T + i * P
                     nc.tensor.matmul_mx(
@@ -432,6 +458,7 @@ def tile_layernormmlp_kernel(
 
         for r in range(n_jobs):
             regroup_upto("S", r + 1 + LOOK_S)
+            stage_upto(r + 3)
             regroup_upto("V", r + 1 + LOOK_V)
             refill()
             if 0 <= r - DG < 8:

@@ -22,10 +22,10 @@ FLOPS = 2 * T * D * F1 + 2 * T * F1 * F2
 JW = 1024
 RING = 12
 BLOCKS = [[0,512],[512,256],[768,256]]
-XS = [640,640,384,640,544,544,544,544,544,544,544,384,384,384,384,384]
+XS = [640,640,384,640,512,512,512,512,512,512,512,384,384,384,384,384]
 QSPLIT = {15: [[0,1],[1,2],[2,3],[3,4]]}
 LOOK_S = 1
-PE_JOBS = [1, 2, 3, 4, 5, 6, 7]
+PE_JOBS = [1, 2, 3, 4, 5, 6, 7, 8, 9, 10]
 STAGED = 768
 LOOK_V = 1
 DG = 1
@@ -196,17 +196,18 @@ def tile_layernormmlp_kernel(
             if eng == "S" and r in PE_JOBS and a == STAGED:
                 st = stage.pop(r)
                 nc.scalar.copy(
-                    out=grp[r][:, 512:JW, :].rearrange("p (t w) j -> p t (w j)", t=4)[:, :, 256:512],
-                    in_=st[:].rearrange("p t w j -> p t (w j)"),
+                    out=grp[r][:, STAGED:JW, :].rearrange("p w j -> p (w j)"),
+                    in_=st[:].rearrange("p t w j -> p (t w j)"),
                 )
             elif job["kind"] == 1:
-                x0 = (a - width * si) // 16
-                x1 = (b - width * si) // 16
+                nt = 2 if r in PE_JOBS and si == 1 else 4
+                x0 = (a - width * si) // (4 * nt)
+                x1 = (b - width * si) // (4 * nt)
                 dst = grp[r][:, width * si : width * (si + 1), :].rearrange(
                     "p (t x e) j -> p t x j e", t=4, e=4
                 )
                 src = seg_src(job, si).rearrange("p j (x t e) -> p t x j e", t=4, e=4)
-                copy_of[eng](out=dst[:, :, x0:x1], in_=src[:, :, x0:x1])
+                copy_of[eng](out=dst[:, 0:nt, x0:x1], in_=src[:, 0:nt, x0:x1])
             else:
                 regroup_part(
                     copy_of[eng], grp[r][:, a:b, :],
@@ -218,13 +219,16 @@ def tile_layernormmlp_kernel(
         def stage_upto(j):
             while done["staged"] < len(PE_JOBS) and PE_JOBS[done["staged"]] < j:
                 r = PE_JOBS[done["staged"]]
-                st = psum.tile([P, 4, 64, 4], BF16, name="st", tag="bank%d" % (done["staged"] % 2))
-                src = raw[r][:, 4:8, :].rearrange("p j (x t e) -> p t x e j", t=4, e=4)
-                for t in range(4):
-                    nc.tensor.matmul(
-                        out=st[:, t, :, :].rearrange("p (x e) j -> p x e j", e=4),
-                        lhsT=ident_b[:], rhs=src[:, t, 16:32], start=True, stop=True,
-                    )
+                st = psum.tile([P, 2, P, 4], BF16, name="st", tag="bank%d" % (done["staged"] % 2))
+                for t in range(2):
+                    if jobs[r]["kind"] == 1:
+                        src = raw[r][:, 4:8, :].rearrange("p j (x t e) -> p t x e j", t=4, e=4)[:, 2 + t]
+                        dst = st[:, t, :, :].rearrange("p (x e) j -> p x e j", e=4)
+                    else:
+                        w0 = STAGED - 512 + t * P
+                        src = seg_src(jobs[r], 1)[:, :, w0 : w0 + P].rearrange("p j w -> p w j")
+                        dst = st[:, t, :, :]
+                    nc.tensor.matmul(out=dst, lhsT=ident_b[:], rhs=src, start=True, stop=True)
                 stage[r] = st
                 done["staged"] = done["staged"] + 1
 

from contextlib import ExitStack

import concourse.mybir as mybir
from concourse.masks import make_identity

F32 = mybir.dt.float32
BF16 = mybir.dt.bfloat16
U32 = mybir.dt.uint32
U8 = mybir.dt.uint8
FP8X4 = mybir.dt.float8_e4m3fn_x4
ACT = mybir.ActivationFunctionType
ALU = mybir.AluOpType

P = 128
T = 512
D = 1024
F1 = 4096
F2 = 1024
EPS = 1e-3
FLOPS = 2 * T * D * F1 + 2 * T * F1 * F2

JW = 1024
RING = 12
BLOCKS = [[0,512],[512,256],[768,256]]
XS = [640,640,384,640,512,512,512,512,512,512,512,384,384,384,384,384]
QSPLIT = {15: [[0,1],[1,2],[2,3],[3,4]]}
LOOK_S = 1
PE_JOBS = [1, 2, 3, 4, 5, 6, 7, 8, 9, 10]
STAGED = 768
LOOK_V = 1
DG = 1
DH = 3
EV_ON = "SSVVSSVV"
EV_ORDER = [0,2,1,3,4,6,5,7]
V_SEQ = ["pp","pppp","q"]
S_SEQ = ["","",""]
CUTS = {"V": {0: 256}, "S": {0: 256}}
COD_BUFS = 4
Q_COLS = 512
GRP_BUFS = 5
FIN_BEFORE = {}
FIN_AFTER = {14: [[1, 0, 4]], 15: [[0, 0, 4]]}
PINNED = True


def make_jobs():
    jobs = []
    for q in range(8):
        jobs.append({"kind": 1, "width": 512, "segs": [(q, 0), (q, 1)]})
    for bi, (c0, width) in enumerate(BLOCKS):
        per = JW // width
        for g0 in range(0, 8, per):
            jobs.append(
                {"kind": 2, "block": bi, "c0": c0, "width": width,
                 "segs": [(8 + g, g) for g in range(g0, g0 + per)]}
            )
    return jobs


def tile_layernormmlp_kernel(
    tc, inputs, gamma, beta, fc1_kernel, fc1_bias, fc2_kernel, fc2_bias, out
):
    nc = tc.nc
    jobs = make_jobs()
    n_jobs = len(jobs)
    last_use = {}
    for ji, job in enumerate(jobs):
        for k, sub in job["segs"]:
            last_use[k] = ji
    with ExitStack() as ctx:
        const = ctx.enter_context(tc.tile_pool(name="const", bufs=1))
        ring = ctx.enter_context(tc.tile_pool(name="ring", bufs=RING))
        grpp = ctx.enter_context(tc.tile_pool(name="grpp", bufs=GRP_BUFS))
        codp = ctx.enter_context(tc.tile_pool(name="codp", bufs=COD_BUFS))
        hpp = ctx.enter_context(tc.tile_pool(name="hpp", bufs=3))
        hgp = ctx.enter_context(tc.tile_pool(name="hgp", bufs=2))
        outp = ctx.enter_context(tc.tile_pool(name="outp", bufs=8))
        psum = ctx.enter_context(tc.psum_pool(name="psum", bufs=1))
        if PINNED:
            ctx.enter_context(tc.manual_schedule())

        def regroup_part(copy_fn, dst, src):
            copy_fn(
                out=dst.rearrange("p (c i) t -> p c t i", i=4),
                in_=src.rearrange("p t (c i) -> p c t i", i=4),
            )

        def quantise(codes, scales, grouped, cols):
            for a in range(0, cols, min(cols, Q_COLS)):
                b = a + min(cols, Q_COLS)
                nc.vector.quantize_mx(
                    out=codes[:, a:b].bitcast(FP8X4), scales=scales[:, a:b],
                    in_=grouped[:, a:b, :].rearrange("p w t -> p (w t)"),
                )

        ident_b = const.tile([P, P], BF16, name="ident_b")
        make_identity(nc, ident_b[:])
        ident_f = const.tile([P, P], F32, name="ident_f")
        make_identity(nc, ident_f[:])
        eps_t = const.tile([P, 1], F32, name="eps_t")
        nc.vector.memset(eps_t[:], EPS)
        vec = const.tile([P, 512], BF16, name="vec")
        nc.vector.memset(vec[:], 0.0)
        vec_h = const.tile([P, 512], BF16, name="vec_h")

        x_all = ring.tile([P, 4, D], BF16, name="x_all", tag="ring")
        for i in range(4):
            nc.sync.dma_start(out=x_all[:, i, :], in_=inputs[i * P : (i + 1) * P, :])
        nc.scalar.dma_start(out=vec[0:2, :], in_=gamma.rearrange("(r c) -> r c", c=512))
        nc.scalar.dma_start(out=vec[2:4, :], in_=beta.rearrange("(r c) -> r c", c=512))
        nc.scalar.dma_start(out=vec[4:12, :], in_=fc1_bias.rearrange("(r c) -> r c", c=512))
        warm = const.tile([P, 2], F32, name="warm")
        nc.scalar.activation(out=warm[:, 0:1], in_=eps_t[:], func=ACT.Sqrt)

        raw = {}
        done = {"S": 0, "V": 0, "load": 0, "free": 0, "quant": 0, "staged": 0}

        def load(k):
            if k < 8:
                t = ring.tile([P, 8, 512], BF16, name="raw", tag="ring")
                for c in range(2):
                    nc.sync.dma_start(
                        out=t[:, 4 * c : 4 * c + 4, :],
                        in_=fc1_kernel[c * 512 : (c + 1) * 512, k * 512 : (k + 1) * 512].rearrange(
                            "(p j) f -> p j f", j=4
                        ),
                    )
            else:
                g = k - 8
                t = ring.tile([P, 4, F2], BF16, name="raw", tag="ring")
                rows = fc2_kernel[g * 512 : (g + 1) * 512, :].rearrange("(x j e) n -> e x j n", j=4, e=4)
                for e in range(4):
                    nc.sync.dma_start(out=t[e::4, :, :], in_=rows[e])
            raw[k] = t
            done["load"] = k + 1

        def refill():
            while done["load"] < 16:
                freed = done["free"]
                for k in range(done["load"]):
                    if min(jobs_done("S"), jobs_done("V")) > last_use[k]:
                        freed = freed + 1
                if done["load"] + 4 - freed >= RING:
                    break
                load(done["load"])
                if done["load"] == 16:
                    nc.sync.dma_start(out=b2[:], in_=fc2_bias.partition_broadcast(P))

        for k in range(RING - 4):
            load(k)
        b2 = const.tile([P, F2], BF16, name="b2")

        grp = {}
        wc = {}
        ws = {}

        def seg_src(job, si):
            k, sub = job["segs"][si]
            if job["kind"] == 1:
                return raw[k][:, 4 * sub : 4 * sub + 4, :]
            return raw[k][:, :, job["c0"] : job["c0"] + job["width"]]

        def piece_list(is_vector):
            pieces = []
            for r, job in enumerate(jobs):
                width = job["width"]
                cut = CUTS["V" if is_vector else "S"].get(r, 0)
                lo = 0 if is_vector else XS[r]
                hi = XS[r] if is_vector else (STAGED if r in PE_JOBS else JW)
                for si in range(len(job["segs"])):
                    a = max(lo, width * si)
                    b = min(hi, width * (si + 1))
                    while a < b:
                        e = min(b, a + cut) if cut > 0 else b
                        pieces.append((r, si, a, e))
                        a = e
                if not is_vector and r in PE_JOBS:
                    pieces.append((r, 1, STAGED, JW))
            return pieces

        todo = {"S": piece_list(False), "V": piece_list(True)}
        copy_of = {"S": nc.scalar.copy, "V": nc.vector.tensor_copy}

        def jobs_done(eng):
            if done[eng] < len(todo[eng]):
                return todo[eng][done[eng]][0]
            return n_jobs

        def emit(eng):
            r, si, a, b = todo[eng][done[eng]]
            done[eng] = done[eng] + 1
            job = jobs[r]
            width = job["width"]
            if r not in grp:
                grp[r] = grpp.tile([P, JW, 4], BF16, name="grp", tag="grp", align_bytes=64)
            if eng == "S" and r in PE_JOBS and a == STAGED:
                st = stage.pop(r)
                nc.scalar.copy(
                    out=grp[r][:, STAGED:JW, :].rearrange("p w j -> p (w j)"),
                    in_=st[:].rearrange("p t w j -> p (t w j)"),
                )
            elif job["kind"] == 1:
                nt = 2 if r in PE_JOBS and si == 1 else 4
                x0 = (a - width * si) // (4 * nt)
                x1 = (b - width * si) // (4 * nt)
                dst = grp[r][:, width * si : width * (si + 1), :].rearrange(
                    "p (t x e) j -> p t x j e", t=4, e=4
                )
                src = seg_src(job, si).rearrange("p j (x t e) -> p t x j e", t=4, e=4)
                copy_of[eng](out=dst[:, 0:nt, x0:x1], in_=src[:, 0:nt, x0:x1])
            else:
                regroup_part(
                    copy_of[eng], grp[r][:, a:b, :],
                    seg_src(job, si)[:, :, a - width * si : b - width * si],
                )

        stage = {}

        def stage_upto(j):
            while done["staged"] < len(PE_JOBS) and PE_JOBS[done["staged"]] < j:
                r = PE_JOBS[done["staged"]]
                st = psum.tile([P, 2, P, 4], BF16, name="st", tag="bank%d" % (done["staged"] % 2))
                for t in range(2):
                    if jobs[r]["kind"] == 1:
                        src = raw[r][:, 4:8, :].rearrange("p j (x t e) -> p t x e j", t=4, e=4)[:, 2 + t]
                        dst = st[:, t, :, :].rearrange("p (x e) j -> p x e j", e=4)
                    else:
                        w0 = STAGED - 512 + t * P
                        src = seg_src(jobs[r], 1)[:, :, w0 : w0 + P].rearrange("p j w -> p w j")
                        dst = st[:, t, :, :]
                    nc.tensor.matmul(out=dst, lhsT=ident_b[:], rhs=src, start=True, stop=True)
                stage[r] = st
                done["staged"] = done["staged"] + 1

        def run_seq(eng, tokens):
            for ch in tokens:
                if ch == "p":
                    if done[eng] < len(todo[eng]):
                        emit(eng)
                else:
                    w_quant(done["quant"])

        def regroup_upto(eng, j):
            while jobs_done(eng) < min(j, n_jobs):
                emit(eng)

        def w_quant(r):
            regroup_upto("V", r + 1)
            regroup_upto("S", r + 1)
            width = jobs[r]["width"]
            wc[r] = codp.tile([P, JW], U32, name="wc", tag="wc", align_bytes=64)
            ws[r] = codp.tile([P, JW], U8, name="ws", tag="ws", align_bytes=64)
            for s0, s1 in QSPLIT.get(r, [(0, len(jobs[r]["segs"]))]):
                a = s0 * width
                b = s1 * width
                quantise(wc[r][:, a:b], ws[r][:, a:b], grp[r][:, a:b, :], b - a)
            done["quant"] = r + 1

        slot = {0: 0, 2: 1, 1: 2, 3: 3}
        rstd = const.tile([P, 4], F32, name="rstd")
        nmr = const.tile([P, 4], F32, name="nmr")
        nmr1 = const.tile([P, 1], F32, name="nmr1")
        junk = const.tile([P, D], BF16, name="junk")
        sum1 = const.tile([P, 1], F32, name="sum1")
        negmu1 = const.tile([P, 1], F32, name="negmu1")
        ssq1 = const.tile([P, 1], F32, name="ssq1")
        nc.scalar.activation(out=junk[:], in_=x_all[:, 1, :], func=ACT.Identity, accum_out=sum1[:])
        nc.scalar.mul(out=negmu1[:], in_=sum1[:], mul=-1.0 / D)
        nc.scalar.activation(
            out=junk[:], in_=x_all[:, 1, :], func=ACT.Square, bias=negmu1[:, 0:1], scale=1.0,
            accum_out=ssq1[:],
        )

        stats = const.tile([P, 4, 2, 6], F32, name="stats")
        mv = const.tile([P, 4, 2], F32, name="mv")
        vt_ps = psum.tile([P, 8, P], BF16, name="vt_ps", tag="bank7")
        for t in range(4):
            nc.tensor.transpose(vt_ps[:, t, :], vec[:, t::4], ident_b[:])
        vec_t = const.tile([P, 8, 12], F32, name="vec_t")

        def bn(i, h):
            nc.vector.bn_stats(
                out=stats[:, slot[i], h, :], in_=x_all[:, i, h * 512 : (h + 1) * 512]
            )

        def aggr(i):
            nc.vector.bn_aggr(
                out=mv[:, slot[i], :], in_=stats[:, slot[i], :, :].rearrange("p s k -> p (s k)")
            )

        std = const.tile([P, 4], F32, name="std")

        def rs_of(a, b):
            nc.scalar.activation(
                out=std[:, a:b], in_=mv[:, a:b, 1], func=ACT.Sqrt, bias=eps_t[:, 0:1], scale=1.0,
            )

        def nmr_of(a, b):
            nc.vector.scalar_tensor_tensor(
                out=nmr[:, a:b], in0=mv[:, a:b, 0], scalar=-1.0, in1=rstd[:, a:b],
                op0=ALU.mult, op1=ALU.mult,
            )

        bn(0, 0)
        bn(0, 1)
        bn(2, 0)
        aggr(0)
        bn(2, 1)
        bn(3, 0)
        aggr(2)
        nc.scalar.activation(
            out=std[:, 2:3], in_=ssq1[:], func=ACT.Sqrt, bias=eps_t[:, 0:1], scale=1.0 / D
        )
        rs_of(0, 2)
        bn(3, 1)
        nc.vector.reciprocal(out=rstd[:, 0:3], in_=std[:, 0:3])
        nc.scalar.mul(out=nmr1[:], in_=negmu1[:], mul=rstd[:, 2:3])
        nmr_of(0, 2)
        aggr(3)
        nc.vector.tensor_copy(
            out=vec_h[:].rearrange("r (t x e) -> r t x e", t=4, e=4),
            in_=vec[:].rearrange("r (x t e) -> r t x e", t=4, e=4),
        )
        for t in range(4):
            nc.tensor.transpose(vt_ps[:, 4 + t, :], vec_h[:, t * P : (t + 1) * P], ident_b[:])

        ln_ps = []
        for b in range(8):
            ln_b = psum.tile([P, T], F32, name="ln_ps%d" % b, tag="bank%d" % b)
            ln_ps.append(ln_b)
        xh = []
        for half in range(2):
            xh_h = ring.tile([P, 2, D], F32, name="xh", tag="ring")
            xh.append(xh_h)
        for i in (1, 0, 2, 3):
            xh_i = xh[i // 2][:, i % 2, :]
            sc = rstd[:, slot[i] : slot[i] + 1]
            sh = nmr1[:, 0:1] if i == 1 else nmr[:, slot[i] : slot[i] + 1]
            nc.scalar.activation(
                out=xh_i.rearrange("q (c t p) -> q c t p", c=2, t=4),
                in_=x_all[:, i, :].rearrange("q (c p t) -> q c t p", c=2, t=4),
                func=ACT.Identity, scale=sc, bias=sh,
            )
            for b in range(8):
                nc.tensor.transpose(
                    ln_ps[b][:, i * P : (i + 1) * P], xh_i[:, b * P : (b + 1) * P], ident_f[:]
                )
            if i == 1:
                rs_of(3, 4)
                run_seq("V", V_SEQ[0])
                nc.vector.tensor_copy(out=vec_t[:], in_=vt_ps[:, :, 0:12])
                nc.vector.reciprocal(out=rstd[:, 3:4], in_=std[:, 3:4])
                nmr_of(3, 4)
        lnp = ring.tile([P, 8, T], BF16, name="lnp", tag="ring")
        done["free"] = 3
        refill()
        nc.scalar.activation(out=warm[:, 1:2], in_=std[:, 0:1], func=ACT.Gelu_apprx_tanh)
        run_seq("S", S_SEQ[2])
        run_seq("V", V_SEQ[1])
        refill()

        for b in EV_ORDER:
            if EV_ON[b] == "S":
                nc.scalar.activation(
                    out=lnp[:, b, :], in_=ln_ps[b][:], func=ACT.Identity,
                    scale=vec_t[:, b % 4, b // 4 : b // 4 + 1],
                    bias=vec_t[:, b % 4, 2 + b // 4 : 3 + b // 4],
                )
            else:
                nc.vector.tensor_scalar(
                    out=lnp[:, b, :], in0=ln_ps[b][:],
                    scalar1=vec_t[:, b % 4, b // 4 : b // 4 + 1],
                    scalar2=vec_t[:, b % 4, 2 + b // 4 : 3 + b // 4], op0=ALU.mult, op1=ALU.add,
                )
        stage_upto(3)
        lnc = const.tile([P, 2 * T], U32, name="lnc", align_bytes=64)
        lns = const.tile([P, 2 * T], U8, name="lns", align_bytes=64)
        lng = grpp.tile([P, JW, 4], BF16, name="grp", tag="grp", align_bytes=64)
        for g in range(2):
            regroup_part(
                nc.vector.tensor_copy, lng[:, g * T : (g + 1) * T, :], lnp[:, 4 * g : 4 * g + 4, :]
            )
        done["free"] = 4
        refill()
        run_seq("V", V_SEQ[2])
        refill()
        quantise(lnc[:], lns[:], lng[:], 2 * T)

        hc = const.tile([P, 8 * T], U32, name="hc", align_bytes=64)
        hs = const.tile([P, 8 * T], U8, name="hs", align_bytes=64)
        acc1 = {}
        acc2 = {}
        hp = {}
        hg = {}

        def fc1(q):
            for j in range(4):
                acc = psum.tile([P, T], F32, name="acc1", tag="bank%d" % (2 + (4 * q + j) % 6))
                for c in range(2):
                    a = c * 512 + j * P
                    nc.tensor.matmul_mx(
                        out=acc[:],
                        lhsT=wc[q][:, a : a + P].bitcast(FP8X4),
                        lhsT_scale=ws[q][:, a : a + P],
                        rhs=lnc[:, c * T : (c + 1) * T].bitcast(FP8X4),
                        rhs_scale=lns[:, c * T : (c + 1) * T],
                        start=(c == 0),
                        stop=(c == 1),
                    )
                acc1[(q, j)] = acc

        def gelu(q):
            hp[q] = hpp.tile([P, 4, T], BF16, name="hp", tag="hp")
            for j in range(4):
                nc.scalar.activation(
                    out=hp[q][:, j, :], in_=acc1[(q, j)][:], func=ACT.Gelu_apprx_tanh,
                    bias=vec_t[:, 4 + j, 4 + q : 5 + q], scale=1.0,
                )

        def h_regroup(q):
            if q % 2 == 0:
                hg[q // 2] = hgp.tile([P, JW, 4], BF16, name="hg", tag="hg", align_bytes=64)
            regroup_part(
                nc.vector.tensor_copy, hg[q // 2][:, (q % 2) * T : (q % 2 + 1) * T, :], hp[q][:]
            )

        def h_quant(q):
            if q % 2 == 1:
                a = (q - 1) * T
                quantise(hc[:, a : a + 2 * T], hs[:, a : a + 2 * T], hg[q // 2][:], 2 * T)

        def fc2(r):
            job = jobs[r]
            width = job["width"]
            bi = job["block"]
            for si in range(len(job["segs"])):
                g = job["segs"][si][1]
                for i in range(4):
                    if g == 0:
                        acc2[(bi, i)] = psum.tile(
                            [P, width], F32, name="acc2", tag="bank%d" % ((2 + 4 * min(bi, 1) + i) % 8)
                        )
                    a = g * T + i * P
                    nc.tensor.matmul_mx(
                        out=acc2[(bi, i)][:],
                        lhsT=hc[:, a : a + P].bitcast(FP8X4),
                        lhsT_scale=hs[:, a : a + P],
                        rhs=wc[r][:, si * width : (si + 1) * width].bitcast(FP8X4),
                        rhs_scale=ws[r][:, si * width : (si + 1) * width],
                        start=(g == 0),
                        stop=(g == 7),
                    )

        def finish(bi, i0, i1):
            c0, width = BLOCKS[bi]
            for i in range(i0, i1):
                o_sb = outp.tile([P, width], F32, name="o_sb", tag="o_sb")
                nc.vector.tensor_tensor(
                    out=o_sb[:], in0=acc2[(bi, i)][:], in1=b2[:, c0 : c0 + width], op=ALU.add
                )
                nc.sync.dma_start(out=out[i * P : (i + 1) * P, c0 : c0 + width], in_=o_sb[:])

        for r in range(n_jobs):
            regroup_upto("S", r + 1 + LOOK_S)
            stage_upto(r + 3)
            regroup_upto("V", r + 1 + LOOK_V)
            refill()
            if 0 <= r - DG < 8:
                gelu(r - DG)
            if 0 <= r - DH < 8:
                h_regroup(r - DH)
            for bi, i0, i1 in FIN_BEFORE.get(r, []):
                finish(bi, i0, i1)
            if r >= done["quant"]:
                w_quant(r)
            if 0 <= r - DH < 8:
                h_quant(r - DH)
            for bi, i0, i1 in FIN_AFTER.get(r, []):
                finish(bi, i0, i1)
            if r < 8:
                fc1(r)
            else:
                fc2(r)
        finish(2, 0, 4)
